import numpy as np
import ml_dtypes


def mxq(x, axis, fmt="e4m3"):
    dtype, down = {"e4m3": (ml_dtypes.float8_e4m3fn, 7), "e5m2": (ml_dtypes.float8_e5m2, 14)}[fmt]
    v = np.moveaxis(np.asarray(x, np.float32).astype(ml_dtypes.bfloat16).astype(np.float64), axis, -1)
    blocks = v.reshape(v.shape[:-1] + (-1, 32))
    amax = np.abs(blocks).max(-1, keepdims=True)
    byte = np.maximum(np.where(amax > 0, np.frexp(amax)[1] - 1 + 127, 0) - down, 1)
    scale = np.exp2(byte - 127.0)
    codes = (blocks / scale).astype(np.float32).astype(dtype).astype(np.float64)
    return np.moveaxis((codes * scale).reshape(v.shape), -1, axis)


WIDE = False


def mx_kscale(k):
    if not WIDE:
        return np.ones(k)
    levels = np.array([10, -10, 5, -5, 0])
    a = np.random.permutation(np.resize(levels, k // 512 * 4)).reshape(k // 512, 4)
    idx = np.arange(k)
    return np.exp2(a[idx // 512, idx % 128 // 32])


BF16 = ml_dtypes.bfloat16


def bf(x):
    return np.asarray(x, np.float32).astype(BF16)


def f64(x):
    return np.asarray(x).astype(np.float64)


N, IN_DIM, HID, OUT_DIM = 1024, 1024, 512, 256
CAT = 3 * HID


def log_softmax(v):
    d = v - v.max(-1, keepdims=True)
    return d - np.log(np.exp(d).sum(-1, keepdims=True))


def setup_inputs():
    s, t = mx_kscale(HID), mx_kscale(CAT)
    ta, tb, tc = t[:HID], t[HID:2 * HID], t[2 * HID:]
    return {"u1": bf(np.maximum(np.random.standard_normal((N, HID)) * 2.0, 0.0) * s),
            "W2_1": bf(np.random.standard_normal((HID, HID)) * 0.5 / np.sqrt(HID) / s[:, None] * tc),
            "b2_1": bf(np.random.standard_normal(HID) * 0.3 * tc),
            "h": bf(np.random.standard_normal((N, HID)) * ta),
            "h1": bf(np.random.standard_normal((N, HID)) * 0.8 * tb),
            "W_out": bf(np.random.standard_normal((CAT, OUT_DIM)) * 2.0 / np.sqrt(CAT) / t[:, None]),
            "b_out": bf(np.random.standard_normal(OUT_DIM) * 0.3)}


def reference(u1, W2_1, b2_1, h, h1, W_out, b_out):
    h2 = (mxq(f64(u1), 1, "e4m3") @ mxq(f64(W2_1), 0, "e4m3")) + f64(b2_1)
    cat = np.concatenate([f64(h), f64(h1), h2], axis=-1)
    logits = (mxq(cat, 1, "e4m3") @ mxq(f64(W_out), 0, "e4m3")) + f64(b_out)
    return log_softmax(logits)

@@ -1,0 +1,234 @@
+from contextlib import ExitStack
+
+import concourse.mybir as mybir
+from concourse.masks import make_identity
+
+F32 = mybir.dt.float32
+BF16 = mybir.dt.bfloat16
+U32 = mybir.dt.uint32
+U8 = mybir.dt.uint8
+FP8X4 = mybir.dt.float8_e4m3fn_x4
+ALU = mybir.AluOpType
+ACT = mybir.ActivationFunctionType
+AX = mybir.AxisListType
+
+P = 128
+NODES = 1024
+HID = 512
+CLASSES = 256
+TILES = NODES // P
+PAIRS = TILES // 2
+WORDS = HID // 2
+FLOPS = 2 * NODES * HID * HID + 2 * NODES * 3 * HID * CLASSES
+
+
+def tile_gin_pc_kernel(tc, u1, W2_1, b2_1, h, h1, W_out, b_out, out):
+    nc = tc.nc
+    with ExitStack() as ctx:
+        keep = ctx.enter_context(tc.tile_pool(name="keep", bufs=1))
+        psum = ctx.enter_context(tc.psum_pool(name="psum", bufs=1))
+
+        ident = keep.tile([P, P], F32)
+        make_identity(nc, ident[:])
+        ones = keep.tile([P, P], BF16)
+        nc.gpsimd.memset(ones[:], 1.0)
+        bo_rows = keep.tile([P, CLASSES], BF16)
+        nc.gpsimd.memset(bo_rows[:], 0.0)
+
+        w2_raw = keep.tile([P, 4 * HID], BF16)
+        u1_sb = keep.tile([P, TILES * HID], BF16)
+        h_sb = keep.tile([P, TILES * HID], BF16)
+        h1_sb = keep.tile([P, TILES * HID], BF16)
+        wo_raw = keep.tile([P, 12 * CLASSES], BF16)
+        b2_raw = keep.tile([P, 4], BF16)
+
+        def load_half(x_sb, x, half):
+            cols = slice(half * 4 * HID, (half + 1) * 4 * HID)
+            nc.sync.dma_start(out=x_sb[:, cols], in_=x.rearrange("(p i) k -> p (i k)", i=TILES)[:, cols])
+
+        nc.scalar.dma_start(out=b2_raw[:], in_=b2_1.rearrange("(p t) -> p t", t=4))
+        nc.scalar.dma_start(out=bo_rows[0:1, :], in_=b_out.rearrange("(o c) -> o c", o=1))
+        nc.sync.dma_start(
+            out=w2_raw[:].rearrange("q (u e c) -> q u e c", u=2, e=2),
+            in_=W2_1.rearrange("(u q e) c -> q u e c", u=2, e=2),
+        )
+        load_half(u1_sb, u1, 0)
+        load_half(u1_sb, u1, 1)
+        nc.sync.dma_start(
+            out=wo_raw[:, 0 : 8 * CLASSES].rearrange("q (a e c) -> q a e c", a=4, e=2),
+            in_=W_out[0 : 2 * HID, :].rearrange("(a q e) c -> q a e c", a=4, e=2),
+        )
+        nc.sync.dma_start(
+            out=wo_raw[:, 8 * CLASSES : 12 * CLASSES],
+            in_=W_out[2 * HID : 3 * HID, :].rearrange("(q t) c -> q (t c)", t=4),
+        )
+        load_half(h_sb, h, 0)
+        load_half(h1_sb, h1, 0)
+        load_half(h_sb, h, 1)
+        load_half(h1_sb, h1, 1)
+
+        w2_g = keep.tile([P, 4 * HID], BF16, align_bytes=64)
+        w2_c = keep.tile([P, HID], U32, align_bytes=64)
+        w2_s = keep.tile([P, HID], U8, align_bytes=64)
+        wo_g = keep.tile([P, 12 * CLASSES], BF16, align_bytes=64)
+        wo_c = keep.tile([P, 3 * CLASSES], U32, align_bytes=64)
+        wo_s = keep.tile([P, 3 * CLASSES], U8, align_bytes=64)
+        u1_g = keep.tile([P, TILES * HID], BF16, align_bytes=64)
+        u1_c = keep.tile([P, NODES], U32, align_bytes=64)
+        u1_s = keep.tile([P, NODES], U8, align_bytes=64)
+        h_g = keep.tile([P, TILES * HID], BF16, align_bytes=64)
+        h_c = keep.tile([P, NODES], U32, align_bytes=64)
+        h_s = keep.tile([P, NODES], U8, align_bytes=64)
+        h1_g = keep.tile([P, TILES * HID], BF16, align_bytes=64)
+        h1_c = keep.tile([P, NODES], U32, align_bytes=64)
+        h1_s = keep.tile([P, NODES], U8, align_bytes=64)
+        h2_g = keep.tile([P, TILES * HID], BF16, align_bytes=64)
+        h2_c = keep.tile([P, NODES], U32, align_bytes=64)
+        h2_s = keep.tile([P, NODES], U8, align_bytes=64)
+        b2_f = keep.tile([P, 4], F32)
+        bo = keep.tile([P, CLASSES], F32)
+        z = keep.tile([P, TILES * CLASSES], F32)
+        junk = keep.tile([P, CLASSES], F32)
+        negm = keep.tile([P, TILES], F32)
+        ssum = keep.tile([P, TILES], F32)
+        lse = keep.tile([P, TILES], F32)
+        negc = keep.tile([P, TILES], F32)
+
+        def quantise(g, c, s, lo, hi):
+            nc.vector.quantize_mx(out=c[:, lo:hi].bitcast(FP8X4), scales=s[:, lo:hi], in_=g[:, 4 * lo : 4 * hi])
+
+        def transposes(x_sb, pair):
+            tp = psum.tile([P, 2, 2, P], F32, tag="tp", bufs=4)
+            words = x_sb[:].bitcast(F32)
+            for s in range(2):
+                for u in range(2):
+                    col = (2 * pair + s) * WORDS + u * P
+                    nc.tensor.transpose(tp[:, s, u, :], words[:, col : col + P], ident[:])
+            return tp
+
+        def copy_out(engine_copy, tp, g, pair):
+            dst = g[:].bitcast(F32)[:, 2 * pair * WORDS : (2 * pair + 2) * WORDS]
+            engine_copy(
+                out=dst.rearrange("p (s n u) -> p s n u", s=2, u=2),
+                in_=tp[:].rearrange("p s u n -> p s n u"),
+            )
+
+        def stage1(i):
+            hp = psum.tile([P, 4, P], F32, tag="hp", bufs=2)
+            for t in range(4):
+                nc.tensor.matmul_mx(
+                    out=hp[:, t, :],
+                    lhsT=w2_c[:, t * P : (t + 1) * P].bitcast(FP8X4),
+                    lhsT_scale=w2_s[:, t * P : (t + 1) * P],
+                    rhs=u1_c[:, i * P : (i + 1) * P].bitcast(FP8X4),
+                    rhs_scale=u1_s[:, i * P : (i + 1) * P],
+                    start=True,
+                    stop=True,
+                )
+            nc.vector.tensor_tensor(
+                out=h2_g[:, i * HID : (i + 1) * HID].rearrange("p (n t) -> p n t", t=4),
+                in0=hp[:].rearrange("p t n -> p n t"),
+                in1=b2_f[:].unsqueeze(1).to_broadcast([P, P, 4]),
+                op=ALU.add,
+            )
+
+        def stage2(pair):
+            lp = psum.tile([P, 2, CLASSES], F32, tag="lp", bufs=2)
+            for s in range(2):
+                i = 2 * pair + s
+                for g, (c, sc) in enumerate(((h_c, h_s), (h1_c, h1_s), (h2_c, h2_s))):
+                    nc.tensor.matmul_mx(
+                        out=lp[:, s, :],
+                        lhsT=c[:, i * P : (i + 1) * P].bitcast(FP8X4),
+                        lhsT_scale=sc[:, i * P : (i + 1) * P],
+                        rhs=wo_c[:, g * CLASSES : (g + 1) * CLASSES].bitcast(FP8X4),
+                        rhs_scale=wo_s[:, g * CLASSES : (g + 1) * CLASSES],
+                        start=(g == 0),
+                        stop=(g == 2),
+                    )
+            zp = z[:, 2 * pair * CLASSES : (2 * pair + 2) * CLASSES].rearrange("p (s c) -> p s c", s=2)
+            nc.vector.tensor_tensor(
+                out=zp, in0=lp[:], in1=bo[:].unsqueeze(1).to_broadcast([P, 2, CLASSES]), op=ALU.add
+            )
+            nc.vector.tensor_reduce(
+                out=negm[:, 2 * pair : 2 * pair + 2], in_=zp, axis=AX.X, op=ALU.max, negate=True
+            )
+            for s in range(2):
+                i = 2 * pair + s
+                nc.scalar.activation(
+                    out=junk[:],
+                    in_=z[:, i * CLASSES : (i + 1) * CLASSES],
+                    func=ACT.Exp,
+                    bias=negm[:, i : i + 1],
+                    scale=1.0,
+                    accum_out=ssum[:, i : i + 1],
+                )
+
+        nc.vector.tensor_copy(out=b2_f[:], in_=b2_raw[:])
+        bp = psum.tile([P, CLASSES], F32, tag="tp", bufs=4)
+        nc.tensor.matmul(out=bp[:], lhsT=ones[:], rhs=bo_rows[:], start=True, stop=True)
+        nc.scalar.copy(out=bo[:], in_=bp[:])
+
+        nc.vector.tensor_copy(
+            out=w2_g[:].rearrange("p (t2 p2 t) -> p t2 p2 t", t2=4, t=4),
+            in_=w2_raw[:].rearrange("p (t p2 t2) -> p t2 p2 t", t=4, t2=4),
+        )
+        quantise(w2_g, w2_c, w2_s, 0, HID)
+
+        u1_tp = [transposes(u1_sb, pair) for pair in range(PAIRS)]
+        for pair in range(PAIRS):
+            copy_out(nc.scalar.copy, u1_tp[pair], u1_g, pair)
+        quantise(u1_g, u1_c, u1_s, 0, NODES // 2)
+        stage1(0)
+        stage1(1)
+        quantise(u1_g, u1_c, u1_s, NODES // 2, NODES)
+        stage1(2)
+        stage1(3)
+
+        for g in range(3):
+            cols = slice(g * 4 * CLASSES, (g + 1) * 4 * CLASSES)
+            nc.scalar.copy(
+                out=wo_g[:, cols].rearrange("p (c i t) -> p c t i", i=4, t=4),
+                in_=wo_raw[:, cols].rearrange("p (t c i) -> p c t i", t=4, i=4),
+            )
+
+        a_tp = [(transposes(h_sb, pair), transposes(h1_sb, pair)) for pair in range(2)]
+        for pair in range(2):
+            copy_out(nc.scalar.copy, a_tp[pair][0], h_g, pair)
+            copy_out(nc.scalar.copy, a_tp[pair][1], h1_g, pair)
+        stage1(4)
+        quantise(h2_g, h2_c, h2_s, 0, NODES // 2)
+        stage1(5)
+        stage1(6)
+        stage1(7)
+        quantise(wo_g, wo_c, wo_s, 0, 2 * CLASSES)
+        quantise(wo_g, wo_c, wo_s, 2 * CLASSES, 3 * CLASSES)
+        quantise(h_g, h_c, h_s, 0, NODES // 2)
+        quantise(h1_g, h1_c, h1_s, 0, NODES // 2)
+        quantise(h2_g, h2_c, h2_s, NODES // 2, NODES)
+
+        b_tp = [(transposes(h_sb, pair), transposes(h1_sb, pair)) for pair in range(2, 4)]
+        for pair in range(2, 4):
+            copy_out(nc.scalar.copy, b_tp[pair - 2][0], h_g, pair)
+            copy_out(nc.scalar.copy, b_tp[pair - 2][1], h1_g, pair)
+
+        stage2(0)
+        stage2(1)
+        quantise(h_g, h_c, h_s, NODES // 2, NODES)
+        quantise(h1_g, h1_c, h1_s, NODES // 2, NODES)
+        stage2(2)
+        stage2(3)
+
+        nc.scalar.activation(out=lse[:], in_=ssum[:], func=ACT.Ln)
+        nc.vector.tensor_tensor(out=negc[:], in0=negm[:], in1=lse[:], op=ALU.subtract)
+        out_rows = out.rearrange("(p i) c -> p (i c)", i=TILES)
+        on_scalar = (5, 6, 7)
+        for pair in (0, 3, 1, 2):
+            for i in (2 * pair, 2 * pair + 1):
+                zi = z[:, i * CLASSES : (i + 1) * CLASSES]
+                if i in on_scalar:
+                    nc.scalar.activation(out=zi, in_=zi, func=ACT.Identity, bias=negc[:, i : i + 1], scale=1.0)
+                else:
+                    nc.vector.tensor_scalar(out=zi, in0=zi, scalar1=negc[:, i : i + 1], scalar2=None, op0=ALU.add)
+            cols = slice(2 * pair * CLASSES, (2 * pair + 2) * CLASSES)
+            nc.sync.dma_start(out=out_rows[:, cols], in_=z[:, cols])

@@ -26,14 +26,15 @@ def tile_gin_pc_kernel(tc, u1, W2_1, b2_1, h, h1, W_out, b_out, out):
     nc = tc.nc
     with ExitStack() as ctx:
         keep = ctx.enter_context(tc.tile_pool(name="keep", bufs=1))
-        psum = ctx.enter_context(tc.psum_pool(name="psum", bufs=1))
+        psum = ctx.enter_context(tc.psum_pool(name="psum", bufs=8))
+        ctx.enter_context(tc.manual_schedule())
 
         ident = keep.tile([P, P], F32)
         make_identity(nc, ident[:])
         ones = keep.tile([P, P], BF16)
         nc.gpsimd.memset(ones[:], 1.0)
         bo_rows = keep.tile([P, CLASSES], BF16)
-        nc.gpsimd.memset(bo_rows[:], 0.0)
+        nc.vector.memset(bo_rows[:], 0.0)
 
         w2_raw = keep.tile([P, 4 * HID], BF16)
         u1_sb = keep.tile([P, TILES * HID], BF16)
@@ -42,8 +43,8 @@ def tile_gin_pc_kernel(tc, u1, W2_1, b2_1, h, h1, W_out, b_out, out):
         wo_raw = keep.tile([P, 12 * CLASSES], BF16)
         b2_raw = keep.tile([P, 4], BF16)
 
-        def load_half(x_sb, x, half):
-            cols = slice(half * 4 * HID, (half + 1) * 4 * HID)
+        def load_tiles(x_sb, x, lo, hi):
+            cols = slice(lo * HID, hi * HID)
             nc.sync.dma_start(out=x_sb[:, cols], in_=x.rearrange("(p i) k -> p (i k)", i=TILES)[:, cols])
 
         nc.scalar.dma_start(out=b2_raw[:], in_=b2_1.rearrange("(p t) -> p t", t=4))
@@ -52,8 +53,9 @@ def tile_gin_pc_kernel(tc, u1, W2_1, b2_1, h, h1, W_out, b_out, out):
             out=w2_raw[:].rearrange("q (u e c) -> q u e c", u=2, e=2),
             in_=W2_1.rearrange("(u q e) c -> q u e c", u=2, e=2),
         )
-        load_half(u1_sb, u1, 0)
-        load_half(u1_sb, u1, 1)
+        load_tiles(u1_sb, u1, 0, 2)
+        load_tiles(u1_sb, u1, 2, 4)
+        load_tiles(u1_sb, u1, 4, 8)
         nc.sync.dma_start(
             out=wo_raw[:, 0 : 8 * CLASSES].rearrange("q (a e c) -> q a e c", a=4, e=2),
             in_=W_out[0 : 2 * HID, :].rearrange("(a q e) c -> q a e c", a=4, e=2),
@@ -62,10 +64,10 @@ def tile_gin_pc_kernel(tc, u1, W2_1, b2_1, h, h1, W_out, b_out, out):
             out=wo_raw[:, 8 * CLASSES : 12 * CLASSES],
             in_=W_out[2 * HID : 3 * HID, :].rearrange("(q t) c -> q (t c)", t=4),
         )
-        load_half(h_sb, h, 0)
-        load_half(h1_sb, h1, 0)
-        load_half(h_sb, h, 1)
-        load_half(h1_sb, h1, 1)
+        load_tiles(h_sb, h, 0, 4)
+        load_tiles(h1_sb, h1, 0, 4)
+        load_tiles(h_sb, h, 4, 8)
+        load_tiles(h1_sb, h1, 4, 8)
 
         w2_g = keep.tile([P, 4 * HID], BF16, align_bytes=64)
         w2_c = keep.tile([P, HID], U32, align_bytes=64)
@@ -98,7 +100,7 @@ def tile_gin_pc_kernel(tc, u1, W2_1, b2_1, h, h1, W_out, b_out, out):
             nc.vector.quantize_mx(out=c[:, lo:hi].bitcast(FP8X4), scales=s[:, lo:hi], in_=g[:, 4 * lo : 4 * hi])
 
         def transposes(x_sb, pair):
-            tp = psum.tile([P, 2, 2, P], F32, tag="tp", bufs=4)
+            tp = psum.tile([P, 2, 2, P], F32, tag="bank")
             words = x_sb[:].bitcast(F32)
             for s in range(2):
                 for u in range(2):
@@ -113,8 +115,8 @@ def tile_gin_pc_kernel(tc, u1, W2_1, b2_1, h, h1, W_out, b_out, out):
                 in_=tp[:].rearrange("p s u n -> p s n u"),
             )
 
-        def stage1(i):
-            hp = psum.tile([P, 4, P], F32, tag="hp", bufs=2)
+        def stage1_mm(i):
+            hp = psum.tile([P, 4, P], F32, tag="bank")
             for t in range(4):
                 nc.tensor.matmul_mx(
                     out=hp[:, t, :],
@@ -125,6 +127,9 @@ def tile_gin_pc_kernel(tc, u1, W2_1, b2_1, h, h1, W_out, b_out, out):
                     start=True,
                     stop=True,
                 )
+            return hp
+
+        def stage1_out(hp, i):
             nc.vector.tensor_tensor(
                 out=h2_g[:, i * HID : (i + 1) * HID].rearrange("p (n t) -> p n t", t=4),
                 in0=hp[:].rearrange("p t n -> p n t"),
@@ -132,8 +137,8 @@ def tile_gin_pc_kernel(tc, u1, W2_1, b2_1, h, h1, W_out, b_out, out):
                 op=ALU.add,
             )
 
-        def stage2(pair):
-            lp = psum.tile([P, 2, CLASSES], F32, tag="lp", bufs=2)
+        def stage2_mm(pair):
+            lp = psum.tile([P, 2, CLASSES], F32, tag="bank")
             for s in range(2):
                 i = 2 * pair + s
                 for g, (c, sc) in enumerate(((h_c, h_s), (h1_c, h1_s), (h2_c, h2_s))):
@@ -146,6 +151,9 @@ def tile_gin_pc_kernel(tc, u1, W2_1, b2_1, h, h1, W_out, b_out, out):
                         start=(g == 0),
                         stop=(g == 2),
                     )
+            return lp
+
+        def logits_max(lp, pair):
             zp = z[:, 2 * pair * CLASSES : (2 * pair + 2) * CLASSES].rearrange("p (s c) -> p s c", s=2)
             nc.vector.tensor_tensor(
                 out=zp, in0=lp[:], in1=bo[:].unsqueeze(1).to_broadcast([P, 2, CLASSES]), op=ALU.add
@@ -153,8 +161,9 @@ def tile_gin_pc_kernel(tc, u1, W2_1, b2_1, h, h1, W_out, b_out, out):
             nc.vector.tensor_reduce(
                 out=negm[:, 2 * pair : 2 * pair + 2], in_=zp, axis=AX.X, op=ALU.max, negate=True
             )
-            for s in range(2):
-                i = 2 * pair + s
+
+        def exps(pair):
+            for i in (2 * pair, 2 * pair + 1):
                 nc.scalar.activation(
                     out=junk[:],
                     in_=z[:, i * CLASSES : (i + 1) * CLASSES],
@@ -164,11 +173,6 @@ def tile_gin_pc_kernel(tc, u1, W2_1, b2_1, h, h1, W_out, b_out, out):
                     accum_out=ssum[:, i : i + 1],
                 )
 
-        nc.vector.tensor_copy(out=b2_f[:], in_=b2_raw[:])
-        bp = psum.tile([P, CLASSES], F32, tag="tp", bufs=4)
-        nc.tensor.matmul(out=bp[:], lhsT=ones[:], rhs=bo_rows[:], start=True, stop=True)
-        nc.scalar.copy(out=bo[:], in_=bp[:])
-
         nc.vector.tensor_copy(
             out=w2_g[:].rearrange("p (t2 p2 t) -> p t2 p2 t", t2=4, t=4),
             in_=w2_raw[:].rearrange("p (t p2 t2) -> p t2 p2 t", t=4, t2=4),
@@ -176,48 +180,65 @@ def tile_gin_pc_kernel(tc, u1, W2_1, b2_1, h, h1, W_out, b_out, out):
         quantise(w2_g, w2_c, w2_s, 0, HID)
 
         u1_tp = [transposes(u1_sb, pair) for pair in range(PAIRS)]
-        for pair in range(PAIRS):
-            copy_out(nc.scalar.copy, u1_tp[pair], u1_g, pair)
-        quantise(u1_g, u1_c, u1_s, 0, NODES // 2)
-        stage1(0)
-        stage1(1)
-        quantise(u1_g, u1_c, u1_s, NODES // 2, NODES)
-        stage1(2)
-        stage1(3)
-
+        copy_out(nc.scalar.copy, u1_tp[0], u1_g, 0)
+        quantise(u1_g, u1_c, u1_s, 0, 2 * P)
+        copy_out(nc.scalar.copy, u1_tp[1], u1_g, 1)
+        nc.vector.tensor_copy(out=b2_f[:], in_=b2_raw[:])
+        quantise(u1_g, u1_c, u1_s, 2 * P, 4 * P)
+        hps = [stage1_mm(0), stage1_mm(1)]
+        copy_out(nc.scalar.copy, u1_tp[2], u1_g, 2)
+        copy_out(nc.scalar.copy, u1_tp[3], u1_g, 3)
+        stage1_out(hps[0], 0)
+        stage1_out(hps[1], 1)
+        quantise(u1_g, u1_c, u1_s, 4 * P, 8 * P)
+        bp = psum.tile([P, CLASSES], F32, tag="bank")
+        nc.tensor.matmul(out=bp[:], lhsT=ones[:], rhs=bo_rows[:], start=True, stop=True)
+        nc.scalar.copy(out=bo[:], in_=bp[:])
+        for i in range(2, TILES):
+            hps.append(stage1_mm(i))
         for g in range(3):
             cols = slice(g * 4 * CLASSES, (g + 1) * 4 * CLASSES)
             nc.scalar.copy(
                 out=wo_g[:, cols].rearrange("p (c i t) -> p c t i", i=4, t=4),
                 in_=wo_raw[:, cols].rearrange("p (t c i) -> p c t i", t=4, i=4),
             )
+        for i in range(2, 5):
+            stage1_out(hps[i], i)
+        quantise(h2_g, h2_c, h2_s, 0, 4 * P)
+        for i in range(5, TILES):
+            stage1_out(hps[i], i)
 
-        a_tp = [(transposes(h_sb, pair), transposes(h1_sb, pair)) for pair in range(2)]
+        x_tp = {}
         for pair in range(2):
-            copy_out(nc.scalar.copy, a_tp[pair][0], h_g, pair)
-            copy_out(nc.scalar.copy, a_tp[pair][1], h1_g, pair)
-        stage1(4)
-        quantise(h2_g, h2_c, h2_s, 0, NODES // 2)
-        stage1(5)
-        stage1(6)
-        stage1(7)
+            x_tp[(0, pair)] = transposes(h_sb, pair)
+            x_tp[(1, pair)] = transposes(h1_sb, pair)
+        for pair in range(2):
+            copy_out(nc.scalar.copy, x_tp[(0, pair)], h_g, pair)
+            copy_out(nc.scalar.copy, x_tp[(1, pair)], h1_g, pair)
         quantise(wo_g, wo_c, wo_s, 0, 2 * CLASSES)
         quantise(wo_g, wo_c, wo_s, 2 * CLASSES, 3 * CLASSES)
-        quantise(h_g, h_c, h_s, 0, NODES // 2)
-        quantise(h1_g, h1_c, h1_s, 0, NODES // 2)
-        quantise(h2_g, h2_c, h2_s, NODES // 2, NODES)
-
-        b_tp = [(transposes(h_sb, pair), transposes(h1_sb, pair)) for pair in range(2, 4)]
+        quantise(h2_g, h2_c, h2_s, 4 * P, 8 * P)
         for pair in range(2, 4):
-            copy_out(nc.scalar.copy, b_tp[pair - 2][0], h_g, pair)
-            copy_out(nc.scalar.copy, b_tp[pair - 2][1], h1_g, pair)
-
-        stage2(0)
-        stage2(1)
-        quantise(h_g, h_c, h_s, NODES // 2, NODES)
-        quantise(h1_g, h1_c, h1_s, NODES // 2, NODES)
-        stage2(2)
-        stage2(3)
+            x_tp[(0, pair)] = transposes(h_sb, pair)
+            x_tp[(1, pair)] = transposes(h1_sb, pair)
+        quantise(h_g, h_c, h_s, 0, 4 * P)
+        quantise(h1_g, h1_c, h1_s, 0, 4 * P)
+        lps = [stage2_mm(0), stage2_mm(1)]
+        for pair in range(2, 4):
+            copy_out(nc.scalar.copy, x_tp[(0, pair)], h_g, pair)
+            copy_out(nc.scalar.copy, x_tp[(1, pair)], h1_g, pair)
+        logits_max(lps[0], 0)
+        exps(0)
+        logits_max(lps[1], 1)
+        exps(1)
+        quantise(h_g, h_c, h_s, 4 * P, 8 * P)
+        quantise(h1_g, h1_c, h1_s, 4 * P, 8 * P)
+        lps.append(stage2_mm(2))
+        lps.append(stage2_mm(3))
+        logits_max(lps[2], 2)
+        exps(2)
+        logits_max(lps[3], 3)
+        exps(3)
 
         nc.scalar.activation(out=lse[:], in_=ssum[:], func=ACT.Ln)
         nc.vector.tensor_tensor(out=negc[:], in0=negm[:], in1=lse[:], op=ALU.subtract)

@@ -87,14 +87,12 @@ def tile_gin_pc_kernel(tc, u1, W2_1, b2_1, h, h1, W_out, b_out, out):
         h2_g = keep.tile([P, TILES * HID], BF16, align_bytes=64)
         h2_c = keep.tile([P, NODES], U32, align_bytes=64)
         h2_s = keep.tile([P, NODES], U8, align_bytes=64)
-        b2_f = keep.tile([P, 4], F32)
         bo = keep.tile([P, CLASSES], F32)
         z = keep.tile([P, TILES * CLASSES], F32)
         junk = keep.tile([P, CLASSES], F32)
         negm = keep.tile([P, TILES], F32)
         ssum = keep.tile([P, TILES], F32)
         lse = keep.tile([P, TILES], F32)
-        negc = keep.tile([P, TILES], F32)
 
         def quantise(g, c, s, lo, hi):
             nc.vector.quantize_mx(out=c[:, lo:hi].bitcast(FP8X4), scales=s[:, lo:hi], in_=g[:, 4 * lo : 4 * hi])
@@ -133,7 +131,7 @@ def tile_gin_pc_kernel(tc, u1, W2_1, b2_1, h, h1, W_out, b_out, out):
             nc.vector.tensor_tensor(
                 out=h2_g[:, i * HID : (i + 1) * HID].rearrange("p (n t) -> p n t", t=4),
                 in0=hp[:].rearrange("p t n -> p n t"),
-                in1=b2_f[:].unsqueeze(1).to_broadcast([P, P, 4]),
+                in1=b2_raw[:].unsqueeze(1).to_broadcast([P, P, 4]),
                 op=ALU.add,
             )
 
@@ -173,83 +171,83 @@ def tile_gin_pc_kernel(tc, u1, W2_1, b2_1, h, h1, W_out, b_out, out):
                     accum_out=ssum[:, i : i + 1],
                 )
 
-        nc.vector.tensor_copy(
-            out=w2_g[:].rearrange("p (t2 p2 t) -> p t2 p2 t", t2=4, t=4),
-            in_=w2_raw[:].rearrange("p (t p2 t2) -> p t2 p2 t", t=4, t2=4),
-        )
+        w2_dst = w2_g[:].rearrange("p (t2 p2 t) -> p t2 p2 t", t2=4, t=4)
+        w2_src = w2_raw[:].rearrange("p (t p2 t2) -> p t2 p2 t", t=4, t2=4)
+        nc.vector.tensor_copy(out=w2_dst[:, 0:3], in_=w2_src[:, 0:3])
+        nc.scalar.copy(out=w2_dst[:, 3], in_=w2_src[:, 3])
         quantise(w2_g, w2_c, w2_s, 0, HID)
 
-        u1_tp = [transposes(u1_sb, pair) for pair in range(PAIRS)]
-        copy_out(nc.scalar.copy, u1_tp[0], u1_g, 0)
-        quantise(u1_g, u1_c, u1_s, 0, 2 * P)
-        copy_out(nc.scalar.copy, u1_tp[1], u1_g, 1)
-        nc.vector.tensor_copy(out=b2_f[:], in_=b2_raw[:])
-        quantise(u1_g, u1_c, u1_s, 2 * P, 4 * P)
-        hps = [stage1_mm(0), stage1_mm(1)]
-        copy_out(nc.scalar.copy, u1_tp[2], u1_g, 2)
-        copy_out(nc.scalar.copy, u1_tp[3], u1_g, 3)
-        stage1_out(hps[0], 0)
-        stage1_out(hps[1], 1)
-        quantise(u1_g, u1_c, u1_s, 4 * P, 8 * P)
-        bp = psum.tile([P, CLASSES], F32, tag="bank")
-        nc.tensor.matmul(out=bp[:], lhsT=ones[:], rhs=bo_rows[:], start=True, stop=True)
-        nc.scalar.copy(out=bo[:], in_=bp[:])
-        for i in range(2, TILES):
-            hps.append(stage1_mm(i))
-        for g in range(3):
+        def regroup_wo(g):
             cols = slice(g * 4 * CLASSES, (g + 1) * 4 * CLASSES)
             nc.scalar.copy(
                 out=wo_g[:, cols].rearrange("p (c i t) -> p c t i", i=4, t=4),
                 in_=wo_raw[:, cols].rearrange("p (t c i) -> p c t i", t=4, i=4),
             )
-        for i in range(2, 5):
+
+        u1_tp = [transposes(u1_sb, 0), transposes(u1_sb, 1)]
+        copy_out(nc.scalar.copy, u1_tp[0], u1_g, 0)
+        quantise(u1_g, u1_c, u1_s, 0, 2 * P)
+        copy_out(nc.scalar.copy, u1_tp[1], u1_g, 1)
+        quantise(u1_g, u1_c, u1_s, 2 * P, 4 * P)
+        hps = [stage1_mm(i) for i in range(4)]
+        u1_tp.append(transposes(u1_sb, 2))
+        u1_tp.append(transposes(u1_sb, 3))
+        regroup_wo(0)
+        copy_out(nc.scalar.copy, u1_tp[2], u1_g, 2)
+        copy_out(nc.scalar.copy, u1_tp[3], u1_g, 3)
+        for i in range(4):
             stage1_out(hps[i], i)
+        quantise(u1_g, u1_c, u1_s, 4 * P, 8 * P)
         quantise(h2_g, h2_c, h2_s, 0, 4 * P)
-        for i in range(5, TILES):
+        bp = psum.tile([P, CLASSES], F32, tag="bank")
+        nc.tensor.matmul(out=bp[:], lhsT=ones[:], rhs=bo_rows[:], start=True, stop=True)
+        nc.scalar.copy(out=bo[:], in_=bp[:])
+        for i in range(4, TILES):
+            hps.append(stage1_mm(i))
+        regroup_wo(1)
+        regroup_wo(2)
+        for i in range(4, TILES):
             stage1_out(hps[i], i)
 
         x_tp = {}
-        for pair in range(2):
+        for pair in range(PAIRS):
             x_tp[(0, pair)] = transposes(h_sb, pair)
             x_tp[(1, pair)] = transposes(h1_sb, pair)
-        for pair in range(2):
+        for pair in range(PAIRS):
             copy_out(nc.scalar.copy, x_tp[(0, pair)], h_g, pair)
             copy_out(nc.scalar.copy, x_tp[(1, pair)], h1_g, pair)
         quantise(wo_g, wo_c, wo_s, 0, 2 * CLASSES)
-        quantise(wo_g, wo_c, wo_s, 2 * CLASSES, 3 * CLASSES)
         quantise(h2_g, h2_c, h2_s, 4 * P, 8 * P)
-        for pair in range(2, 4):
-            x_tp[(0, pair)] = transposes(h_sb, pair)
-            x_tp[(1, pair)] = transposes(h1_sb, pair)
-        quantise(h_g, h_c, h_s, 0, 4 * P)
-        quantise(h1_g, h1_c, h1_s, 0, 4 * P)
-        lps = [stage2_mm(0), stage2_mm(1)]
-        for pair in range(2, 4):
-            copy_out(nc.scalar.copy, x_tp[(0, pair)], h_g, pair)
-            copy_out(nc.scalar.copy, x_tp[(1, pair)], h1_g, pair)
+        quantise(wo_g, wo_c, wo_s, 2 * CLASSES, 3 * CLASSES)
+
+        def quantise_pair(pair):
+            quantise(h_g, h_c, h_s, 2 * pair * P, (2 * pair + 2) * P)
+            quantise(h1_g, h1_c, h1_s, 2 * pair * P, (2 * pair + 2) * P)
+
+        quantise_pair(0)
+        quantise_pair(1)
+        quantise_pair(2)
+        lps = [stage2_mm(0), stage2_mm(1), stage2_mm(2)]
         logits_max(lps[0], 0)
         exps(0)
-        logits_max(lps[1], 1)
-        exps(1)
-        quantise(h_g, h_c, h_s, 4 * P, 8 * P)
-        quantise(h1_g, h1_c, h1_s, 4 * P, 8 * P)
-        lps.append(stage2_mm(2))
+        quantise_pair(3)
         lps.append(stage2_mm(3))
-        logits_max(lps[2], 2)
-        exps(2)
-        logits_max(lps[3], 3)
-        exps(3)
+        for pair in range(1, PAIRS):
+            logits_max(lps[pair], pair)
+            exps(pair)
 
         nc.scalar.activation(out=lse[:], in_=ssum[:], func=ACT.Ln)
-        nc.vector.tensor_tensor(out=negc[:], in0=negm[:], in1=lse[:], op=ALU.subtract)
         out_rows = out.rearrange("(p i) c -> p (i c)", i=TILES)
-        on_scalar = (5, 6, 7)
-        for pair in (0, 3, 1, 2):
+        for pair in range(PAIRS):
             for i in (2 * pair, 2 * pair + 1):
                 zi = z[:, i * CLASSES : (i + 1) * CLASSES]
-                if i in on_scalar:
-                    nc.scalar.activation(out=zi, in_=zi, func=ACT.Identity, bias=negc[:, i : i + 1], scale=1.0)
-                else:
-                    nc.vector.tensor_scalar(out=zi, in0=zi, scalar1=negc[:, i : i + 1], scalar2=None, op0=ALU.add)
+                nc.vector.tensor_scalar(
+                    out=zi,
+                    in0=zi,
+                    scalar1=negm[:, i : i + 1],
+                    scalar2=lse[:, i : i + 1],
+                    op0=ALU.add,
+                    op1=ALU.subtract,
+                )
             cols = slice(2 * pair * CLASSES, (2 * pair + 2) * CLASSES)
             nc.sync.dma_start(out=out_rows[:, cols], in_=z[:, cols])

@@ -185,28 +185,29 @@ def tile_gin_pc_kernel(tc, u1, W2_1, b2_1, h, h1, W_out, b_out, out):
             )
 
         u1_tp = [transposes(u1_sb, 0), transposes(u1_sb, 1)]
+        bp = psum.tile([P, CLASSES], F32, tag="bank")
+        nc.tensor.matmul(out=bp[:], lhsT=ones[:], rhs=bo_rows[:], start=True, stop=True)
+        u1_tp.append(transposes(u1_sb, 2))
+        u1_tp.append(transposes(u1_sb, 3))
         copy_out(nc.scalar.copy, u1_tp[0], u1_g, 0)
         quantise(u1_g, u1_c, u1_s, 0, 2 * P)
         copy_out(nc.scalar.copy, u1_tp[1], u1_g, 1)
         quantise(u1_g, u1_c, u1_s, 2 * P, 4 * P)
-        hps = [stage1_mm(i) for i in range(4)]
-        u1_tp.append(transposes(u1_sb, 2))
-        u1_tp.append(transposes(u1_sb, 3))
-        regroup_wo(0)
         copy_out(nc.scalar.copy, u1_tp[2], u1_g, 2)
         copy_out(nc.scalar.copy, u1_tp[3], u1_g, 3)
-        for i in range(4):
-            stage1_out(hps[i], i)
-        quantise(u1_g, u1_c, u1_s, 4 * P, 8 * P)
-        quantise(h2_g, h2_c, h2_s, 0, 4 * P)
-        bp = psum.tile([P, CLASSES], F32, tag="bank")
-        nc.tensor.matmul(out=bp[:], lhsT=ones[:], rhs=bo_rows[:], start=True, stop=True)
         nc.scalar.copy(out=bo[:], in_=bp[:])
+        hps = [stage1_mm(i) for i in range(4)]
+        stage1_out(hps[0], 0)
+        stage1_out(hps[1], 1)
+        quantise(u1_g, u1_c, u1_s, 4 * P, 8 * P)
         for i in range(4, TILES):
             hps.append(stage1_mm(i))
-        regroup_wo(1)
-        regroup_wo(2)
-        for i in range(4, TILES):
+        for g in range(3):
+            regroup_wo(g)
+        for i in range(2, 5):
+            stage1_out(hps[i], i)
+        quantise(h2_g, h2_c, h2_s, 0, 4 * P)
+        for i in range(5, TILES):
             stage1_out(hps[i], i)
 
         x_tp = {}
@@ -224,10 +225,10 @@ def tile_gin_pc_kernel(tc, u1, W2_1, b2_1, h, h1, W_out, b_out, out):
             quantise(h_g, h_c, h_s, 2 * pair * P, (2 * pair + 2) * P)
             quantise(h1_g, h1_c, h1_s, 2 * pair * P, (2 * pair + 2) * P)
 
-        quantise_pair(0)
-        quantise_pair(1)
-        quantise_pair(2)
-        lps = [stage2_mm(0), stage2_mm(1), stage2_mm(2)]
+        lps = []
+        for pair in range(3):
+            quantise_pair(pair)
+            lps.append(stage2_mm(pair))
         logits_max(lps[0], 0)
         exps(0)
         quantise_pair(3)
@@ -235,7 +236,6 @@ def tile_gin_pc_kernel(tc, u1, W2_1, b2_1, h, h1, W_out, b_out, out):
         for pair in range(1, PAIRS):
             logits_max(lps[pair], pair)
             exps(pair)
-
         nc.scalar.activation(out=lse[:], in_=ssum[:], func=ACT.Ln)
         out_rows = out.rearrange("(p i) c -> p (i c)", i=TILES)
         for pair in range(PAIRS):

@@ -26,7 +26,7 @@ def tile_gin_pc_kernel(tc, u1, W2_1, b2_1, h, h1, W_out, b_out, out):
     nc = tc.nc
     with ExitStack() as ctx:
         keep = ctx.enter_context(tc.tile_pool(name="keep", bufs=1))
-        psum = ctx.enter_context(tc.psum_pool(name="psum", bufs=8))
+        psum = ctx.enter_context(tc.psum_pool(name="psum", bufs=7))
         ctx.enter_context(tc.manual_schedule())
 
         ident = keep.tile([P, P], F32)
@@ -35,6 +35,15 @@ def tile_gin_pc_kernel(tc, u1, W2_1, b2_1, h, h1, W_out, b_out, out):
         nc.gpsimd.memset(ones[:], 1.0)
         bo_rows = keep.tile([P, CLASSES], BF16)
         nc.vector.memset(bo_rows[:], 0.0)
+        warm_rhs = keep.tile([P, CLASSES], F32)
+        nc.vector.memset(warm_rhs[:], 0.0)
+        warm_out = psum.tile([P, CLASSES], F32, tag="warm", bufs=1)
+
+        def keep_warm(times):
+            for rep in range(times):
+                nc.tensor.matmul(out=warm_out[:], lhsT=ident[:], rhs=warm_rhs[:], start=True, stop=True)
+
+        keep_warm(2)
 
         w2_raw = keep.tile([P, 4 * HID], BF16)
         u1_sb = keep.tile([P, TILES * HID], BF16)
@@ -187,6 +196,7 @@ def tile_gin_pc_kernel(tc, u1, W2_1, b2_1, h, h1, W_out, b_out, out):
         u1_tp = [transposes(u1_sb, 0), transposes(u1_sb, 1)]
         bp = psum.tile([P, CLASSES], F32, tag="bank")
         nc.tensor.matmul(out=bp[:], lhsT=ones[:], rhs=bo_rows[:], start=True, stop=True)
+        keep_warm(1)
         u1_tp.append(transposes(u1_sb, 2))
         u1_tp.append(transposes(u1_sb, 3))
         copy_out(nc.scalar.copy, u1_tp[0], u1_g, 0)
@@ -197,11 +207,13 @@ def tile_gin_pc_kernel(tc, u1, W2_1, b2_1, h, h1, W_out, b_out, out):
         copy_out(nc.scalar.copy, u1_tp[3], u1_g, 3)
         nc.scalar.copy(out=bo[:], in_=bp[:])
         hps = [stage1_mm(i) for i in range(4)]
+        keep_warm(1)
         stage1_out(hps[0], 0)
         stage1_out(hps[1], 1)
         quantise(u1_g, u1_c, u1_s, 4 * P, 8 * P)
         for i in range(4, TILES):
             hps.append(stage1_mm(i))
+        keep_warm(1)
         for g in range(3):
             regroup_wo(g)
         for i in range(2, 5):
@@ -214,6 +226,8 @@ def tile_gin_pc_kernel(tc, u1, W2_1, b2_1, h, h1, W_out, b_out, out):
         for pair in range(PAIRS):
             x_tp[(0, pair)] = transposes(h_sb, pair)
             x_tp[(1, pair)] = transposes(h1_sb, pair)
+            if pair % 2 == 1:
+                keep_warm((pair + 1) // 2)
         for pair in range(PAIRS):
             copy_out(nc.scalar.copy, x_tp[(0, pair)], h_g, pair)
             copy_out(nc.scalar.copy, x_tp[(1, pair)], h1_g, pair)
@@ -229,6 +243,8 @@ def tile_gin_pc_kernel(tc, u1, W2_1, b2_1, h, h1, W_out, b_out, out):
         for pair in range(3):
             quantise_pair(pair)
             lps.append(stage2_mm(pair))
+            if pair == 1:
+                keep_warm(1)
         logits_max(lps[0], 0)
         exps(0)
         quantise_pair(3)

@@ -144,6 +144,13 @@ def tile_gin_pc_kernel(tc, u1, W2_1, b2_1, h, h1, W_out, b_out, out):
                 op=ALU.add,
             )
 
+        def stage1_out_scalar(hp, i):
+            dst = h2_g[:, i * HID : (i + 1) * HID].rearrange("p (n t) -> p n t", t=4)
+            for t in range(4):
+                nc.scalar.activation(
+                    out=dst[:, :, t], in_=hp[:, t, :], func=ACT.Identity, bias=b2_raw[:, t : t + 1], scale=1.0
+                )
+
         def stage2_mm(pair):
             lp = psum.tile([P, 2, CLASSES], F32, tag="bank")
             for s in range(2):
@@ -188,9 +195,13 @@ def tile_gin_pc_kernel(tc, u1, W2_1, b2_1, h, h1, W_out, b_out, out):
 
         def regroup_wo(g):
             cols = slice(g * 4 * CLASSES, (g + 1) * 4 * CLASSES)
-            nc.scalar.copy(
-                out=wo_g[:, cols].rearrange("p (c i t) -> p c t i", i=4, t=4),
-                in_=wo_raw[:, cols].rearrange("p (t c i) -> p c t i", t=4, i=4),
+            nc.gpsimd.tensor_scalar(
+                out=wo_g[:, cols].rearrange("p (c t) -> p c t", t=4),
+                in0=wo_raw[:, cols].rearrange("p (t c) -> p c t", t=4),
+                scalar1=1.0,
+                scalar2=0.0,
+                op0=ALU.mult,
+                op1=ALU.add,
             )
 
         u1_tp = [transposes(u1_sb, 0), transposes(u1_sb, 1)]
@@ -209,18 +220,19 @@ def tile_gin_pc_kernel(tc, u1, W2_1, b2_1, h, h1, W_out, b_out, out):
         hps = [stage1_mm(i) for i in range(4)]
         keep_warm(1)
         stage1_out(hps[0], 0)
-        stage1_out(hps[1], 1)
         quantise(u1_g, u1_c, u1_s, 4 * P, 8 * P)
+        stage1_out(hps[1], 1)
         for i in range(4, TILES):
             hps.append(stage1_mm(i))
         keep_warm(1)
         for g in range(3):
             regroup_wo(g)
-        for i in range(2, 5):
+        stage1_out_scalar(hps[2], 2)
+        stage1_out_scalar(hps[6], 6)
+        for i in (3, 4, 5):
             stage1_out(hps[i], i)
         quantise(h2_g, h2_c, h2_s, 0, 4 * P)
-        for i in range(5, TILES):
-            stage1_out(hps[i], i)
+        stage1_out(hps[7], 7)
 
         x_tp = {}
         for pair in range(PAIRS):

@@ -228,10 +228,10 @@ def tile_gin_pc_kernel(tc, u1, W2_1, b2_1, h, h1, W_out, b_out, out):
         for g in range(3):
             regroup_wo(g)
         stage1_out_scalar(hps[2], 2)
-        stage1_out_scalar(hps[6], 6)
         for i in (3, 4, 5):
             stage1_out(hps[i], i)
         quantise(h2_g, h2_c, h2_s, 0, 4 * P)
+        stage1_out(hps[6], 6)
         stage1_out(hps[7], 7)
 
         x_tp = {}

@@ -228,11 +228,10 @@ def tile_gin_pc_kernel(tc, u1, W2_1, b2_1, h, h1, W_out, b_out, out):
         for g in range(3):
             regroup_wo(g)
         stage1_out_scalar(hps[2], 2)
-        for i in (3, 4, 5):
+        stage1_out_scalar(hps[6], 6)
+        for i in (3, 4, 5, 7):
             stage1_out(hps[i], i)
         quantise(h2_g, h2_c, h2_s, 0, 4 * P)
-        stage1_out(hps[6], 6)
-        stage1_out(hps[7], 7)
 
         x_tp = {}
         for pair in range(PAIRS):

from contextlib import ExitStack

import concourse.mybir as mybir
from concourse.masks import make_identity

F32 = mybir.dt.float32
BF16 = mybir.dt.bfloat16
U32 = mybir.dt.uint32
U8 = mybir.dt.uint8
FP8X4 = mybir.dt.float8_e4m3fn_x4
ALU = mybir.AluOpType
ACT = mybir.ActivationFunctionType
AX = mybir.AxisListType

P = 128
NODES = 1024
HID = 512
CLASSES = 256
TILES = NODES // P
PAIRS = TILES // 2
WORDS = HID // 2
FLOPS = 2 * NODES * HID * HID + 2 * NODES * 3 * HID * CLASSES


def tile_gin_pc_kernel(tc, u1, W2_1, b2_1, h, h1, W_out, b_out, out):
    nc = tc.nc
    with ExitStack() as ctx:
        keep = ctx.enter_context(tc.tile_pool(name="keep", bufs=1))
        psum = ctx.enter_context(tc.psum_pool(name="psum", bufs=7))
        ctx.enter_context(tc.manual_schedule())

        ident = keep.tile([P, P], F32)
        make_identity(nc, ident[:])
        ones = keep.tile([P, P], BF16)
        nc.gpsimd.memset(ones[:], 1.0)
        bo_rows = keep.tile([P, CLASSES], BF16)
        nc.vector.memset(bo_rows[:], 0.0)
        warm_rhs = keep.tile([P, CLASSES], F32)
        nc.vector.memset(warm_rhs[:], 0.0)
        warm_out = psum.tile([P, CLASSES], F32, tag="warm", bufs=1)

        def keep_warm(times):
            for rep in range(times):
                nc.tensor.matmul(out=warm_out[:], lhsT=ident[:], rhs=warm_rhs[:], start=True, stop=True)

        keep_warm(2)

        w2_raw = keep.tile([P, 4 * HID], BF16)
        u1_sb = keep.tile([P, TILES * HID], BF16)
        h_sb = keep.tile([P, TILES * HID], BF16)
        h1_sb = keep.tile([P, TILES * HID], BF16)
        wo_raw = keep.tile([P, 12 * CLASSES], BF16)
        b2_raw = keep.tile([P, 4], BF16)

        def load_tiles(x_sb, x, lo, hi):
            cols = slice(lo * HID, hi * HID)
            nc.sync.dma_start(out=x_sb[:, cols], in_=x.rearrange("(p i) k -> p (i k)", i=TILES)[:, cols])

        nc.scalar.dma_start(out=b2_raw[:], in_=b2_1.rearrange("(p t) -> p t", t=4))
        nc.scalar.dma_start(out=bo_rows[0:1, :], in_=b_out.rearrange("(o c) -> o c", o=1))
        nc.sync.dma_start(
            out=w2_raw[:].rearrange("q (u e c) -> q u e c", u=2, e=2),
            in_=W2_1.rearrange("(u q e) c -> q u e c", u=2, e=2),
        )
        load_tiles(u1_sb, u1, 0, 2)
        load_tiles(u1_sb, u1, 2, 4)
        load_tiles(u1_sb, u1, 4, 8)
        nc.sync.dma_start(
            out=wo_raw[:, 0 : 8 * CLASSES].rearrange("q (a e c) -> q a e c", a=4, e=2),
            in_=W_out[0 : 2 * HID, :].rearrange("(a q e) c -> q a e c", a=4, e=2),
        )
        nc.sync.dma_start(
            out=wo_raw[:, 8 * CLASSES : 12 * CLASSES],
            in_=W_out[2 * HID : 3 * HID, :].rearrange("(q t) c -> q (t c)", t=4),
        )
        load_tiles(h_sb, h, 0, 4)
        load_tiles(h1_sb, h1, 0, 4)
        load_tiles(h_sb, h, 4, 8)
        load_tiles(h1_sb, h1, 4, 8)

        w2_g = keep.tile([P, 4 * HID], BF16, align_bytes=64)
        w2_c = keep.tile([P, HID], U32, align_bytes=64)
        w2_s = keep.tile([P, HID], U8, align_bytes=64)
        wo_g = keep.tile([P, 12 * CLASSES], BF16, align_bytes=64)
        wo_c = keep.tile([P, 3 * CLASSES], U32, align_bytes=64)
        wo_s = keep.tile([P, 3 * CLASSES], U8, align_bytes=64)
        u1_g = keep.tile([P, TILES * HID], BF16, align_bytes=64)
        u1_c = keep.tile([P, NODES], U32, align_bytes=64)
        u1_s = keep.tile([P, NODES], U8, align_bytes=64)
        h_g = keep.tile([P, TILES * HID], BF16, align_bytes=64)
        h_c = keep.tile([P, NODES], U32, align_bytes=64)
        h_s = keep.tile([P, NODES], U8, align_bytes=64)
        h1_g = keep.tile([P, TILES * HID], BF16, align_bytes=64)
        h1_c = keep.tile([P, NODES], U32, align_bytes=64)
        h1_s = keep.tile([P, NODES], U8, align_bytes=64)
        h2_g = keep.tile([P, TILES * HID], BF16, align_bytes=64)
        h2_c = keep.tile([P, NODES], U32, align_bytes=64)
        h2_s = keep.tile([P, NODES], U8, align_bytes=64)
        bo = keep.tile([P, CLASSES], F32)
        z = keep.tile([P, TILES * CLASSES], F32)
        junk = keep.tile([P, CLASSES], F32)
        negm = keep.tile([P, TILES], F32)
        ssum = keep.tile([P, TILES], F32)
        lse = keep.tile([P, TILES], F32)

        def quantise(g, c, s, lo, hi):
            nc.vector.quantize_mx(out=c[:, lo:hi].bitcast(FP8X4), scales=s[:, lo:hi], in_=g[:, 4 * lo : 4 * hi])

        def transposes(x_sb, pair):
            tp = psum.tile([P, 2, 2, P], F32, tag="bank")
            words = x_sb[:].bitcast(F32)
            for s in range(2):
                for u in range(2):
                    col = (2 * pair + s) * WORDS + u * P
                    nc.tensor.transpose(tp[:, s, u, :], words[:, col : col + P], ident[:])
            return tp

        def copy_out(engine_copy, tp, g, pair):
            dst = g[:].bitcast(F32)[:, 2 * pair * WORDS : (2 * pair + 2) * WORDS]
            engine_copy(
                out=dst.rearrange("p (s n u) -> p s n u", s=2, u=2),
                in_=tp[:].rearrange("p s u n -> p s n u"),
            )

        def stage1_mm(i):
            hp = psum.tile([P, 4, P], F32, tag="bank")
            for t in range(4):
                nc.tensor.matmul_mx(
                    out=hp[:, t, :],
                    lhsT=w2_c[:, t * P : (t + 1) * P].bitcast(FP8X4),
                    lhsT_scale=w2_s[:, t * P : (t + 1) * P],
                    rhs=u1_c[:, i * P : (i + 1) * P].bitcast(FP8X4),
                    rhs_scale=u1_s[:, i * P : (i + 1) * P],
                    start=True,
                    stop=True,
                )
            return hp

        def stage1_out(hp, i):
            nc.vector.tensor_tensor(
                out=h2_g[:, i * HID : (i + 1) * HID].rearrange("p (n t) -> p n t", t=4),
                in0=hp[:].rearrange("p t n -> p n t"),
                in1=b2_raw[:].unsqueeze(1).to_broadcast([P, P, 4]),
                op=ALU.add,
            )

        def stage1_out_scalar(hp, i):
            dst = h2_g[:, i * HID : (i + 1) * HID].rearrange("p (n t) -> p n t", t=4)
            for t in range(4):
                nc.scalar.activation(
                    out=dst[:, :, t], in_=hp[:, t, :], func=ACT.Identity, bias=b2_raw[:, t : t + 1], scale=1.0
                )

        def stage2_mm(pair):
            lp = psum.tile([P, 2, CLASSES], F32, tag="bank")
            for s in range(2):
                i = 2 * pair + s
                for g, (c, sc) in enumerate(((h_c, h_s), (h1_c, h1_s), (h2_c, h2_s))):
                    nc.tensor.matmul_mx(
                        out=lp[:, s, :],
                        lhsT=c[:, i * P : (i + 1) * P].bitcast(FP8X4),
                        lhsT_scale=sc[:, i * P : (i + 1) * P],
                        rhs=wo_c[:, g * CLASSES : (g + 1) * CLASSES].bitcast(FP8X4),
                        rhs_scale=wo_s[:, g * CLASSES : (g + 1) * CLASSES],
                        start=(g == 0),
                        stop=(g == 2),
                    )
            return lp

        def logits_max(lp, pair):
            zp = z[:, 2 * pair * CLASSES : (2 * pair + 2) * CLASSES].rearrange("p (s c) -> p s c", s=2)
            nc.vector.tensor_tensor(
                out=zp, in0=lp[:], in1=bo[:].unsqueeze(1).to_broadcast([P, 2, CLASSES]), op=ALU.add
            )
            nc.vector.tensor_reduce(
                out=negm[:, 2 * pair : 2 * pair + 2], in_=zp, axis=AX.X, op=ALU.max, negate=True
            )

        def exps(pair):
            for i in (2 * pair, 2 * pair + 1):
                nc.scalar.activation(
                    out=junk[:],
                    in_=z[:, i * CLASSES : (i + 1) * CLASSES],
                    func=ACT.Exp,
                    bias=negm[:, i : i + 1],
                    scale=1.0,
                    accum_out=ssum[:, i : i + 1],
                )

        w2_dst = w2_g[:].rearrange("p (t2 p2 t) -> p t2 p2 t", t2=4, t=4)
        w2_src = w2_raw[:].rearrange("p (t p2 t2) -> p t2 p2 t", t=4, t2=4)
        nc.vector.tensor_copy(out=w2_dst[:, 0:3], in_=w2_src[:, 0:3])
        nc.scalar.copy(out=w2_dst[:, 3], in_=w2_src[:, 3])
        quantise(w2_g, w2_c, w2_s, 0, HID)

        def regroup_wo(g):
            cols = slice(g * 4 * CLASSES, (g + 1) * 4 * CLASSES)
            nc.gpsimd.tensor_scalar(
                out=wo_g[:, cols].rearrange("p (c t) -> p c t", t=4),
                in0=wo_raw[:, cols].rearrange("p (t c) -> p c t", t=4),
                scalar1=1.0,
                scalar2=0.0,
                op0=ALU.mult,
                op1=ALU.add,
            )

        u1_tp = [transposes(u1_sb, 0), transposes(u1_sb, 1)]
        bp = psum.tile([P, CLASSES], F32, tag="bank")
        nc.tensor.matmul(out=bp[:], lhsT=ones[:], rhs=bo_rows[:], start=True, stop=True)
        keep_warm(1)
        u1_tp.append(transposes(u1_sb, 2))
        u1_tp.append(transposes(u1_sb, 3))
        copy_out(nc.scalar.copy, u1_tp[0], u1_g, 0)
        quantise(u1_g, u1_c, u1_s, 0, 2 * P)
        copy_out(nc.scalar.copy, u1_tp[1], u1_g, 1)
        quantise(u1_g, u1_c, u1_s, 2 * P, 4 * P)
        copy_out(nc.scalar.copy, u1_tp[2], u1_g, 2)
        copy_out(nc.scalar.copy, u1_tp[3], u1_g, 3)
        nc.scalar.copy(out=bo[:], in_=bp[:])
        hps = [stage1_mm(i) for i in range(4)]
        keep_warm(1)
        stage1_out(hps[0], 0)
        quantise(u1_g, u1_c, u1_s, 4 * P, 8 * P)
        stage1_out(hps[1], 1)
        for i in range(4, TILES):
            hps.append(stage1_mm(i))
        keep_warm(1)
        for g in range(3):
            regroup_wo(g)
        stage1_out_scalar(hps[2], 2)
        stage1_out_scalar(hps[6], 6)
        for i in (3, 4, 5, 7):
            stage1_out(hps[i], i)
        quantise(h2_g, h2_c, h2_s, 0, 4 * P)

        x_tp = {}
        for pair in range(PAIRS):
            x_tp[(0, pair)] = transposes(h_sb, pair)
            x_tp[(1, pair)] = transposes(h1_sb, pair)
            if pair % 2 == 1:
                keep_warm((pair + 1) // 2)
        for pair in range(PAIRS):
            copy_out(nc.scalar.copy, x_tp[(0, pair)], h_g, pair)
            copy_out(nc.scalar.copy, x_tp[(1, pair)], h1_g, pair)
        quantise(wo_g, wo_c, wo_s, 0, 2 * CLASSES)
        quantise(h2_g, h2_c, h2_s, 4 * P, 8 * P)
        quantise(wo_g, wo_c, wo_s, 2 * CLASSES, 3 * CLASSES)

        def quantise_pair(pair):
            quantise(h_g, h_c, h_s, 2 * pair * P, (2 * pair + 2) * P)
            quantise(h1_g, h1_c, h1_s, 2 * pair * P, (2 * pair + 2) * P)

        lps = []
        for pair in range(3):
            quantise_pair(pair)
            lps.append(stage2_mm(pair))
            if pair == 1:
                keep_warm(1)
        logits_max(lps[0], 0)
        exps(0)
        quantise_pair(3)
        lps.append(stage2_mm(3))
        for pair in range(1, PAIRS):
            logits_max(lps[pair], pair)
            exps(pair)
        nc.scalar.activation(out=lse[:], in_=ssum[:], func=ACT.Ln)
        out_rows = out.rearrange("(p i) c -> p (i c)", i=TILES)
        for pair in range(PAIRS):
            for i in (2 * pair, 2 * pair + 1):
                zi = z[:, i * CLASSES : (i + 1) * CLASSES]
                nc.vector.tensor_scalar(
                    out=zi,
                    in0=zi,
                    scalar1=negm[:, i : i + 1],
                    scalar2=lse[:, i : i + 1],
                    op0=ALU.add,
                    op1=ALU.subtract,
                )
            cols = slice(2 * pair * CLASSES, (2 * pair + 2) * CLASSES)
            nc.sync.dma_start(out=out_rows[:, cols], in_=z[:, cols])
